import numpy as np
import ml_dtypes


def mxq(x, axis, fmt="e4m3"):
    dtype, down = {"e4m3": (ml_dtypes.float8_e4m3fn, 7), "e5m2": (ml_dtypes.float8_e5m2, 14)}[fmt]
    v = np.moveaxis(np.asarray(x, np.float32).astype(ml_dtypes.bfloat16).astype(np.float64), axis, -1)
    blocks = v.reshape(v.shape[:-1] + (-1, 32))
    amax = np.abs(blocks).max(-1, keepdims=True)
    byte = np.maximum(np.where(amax > 0, np.frexp(amax)[1] - 1 + 127, 0) - down, 1)
    scale = np.exp2(byte - 127.0)
    codes = (blocks / scale).astype(np.float32).astype(dtype).astype(np.float64)
    return np.moveaxis((codes * scale).reshape(v.shape), -1, axis)


WIDE = False


def mx_kscale(k):
    if not WIDE:
        return np.ones(k)
    levels = np.array([10, -10, 5, -5, 0])
    if k % 512:
        return np.exp2(np.random.permutation(np.resize(levels, k // 32))).repeat(32)
    a = np.empty((k // 512, 16))
    for p in range(k // 512):
        a[p, :8] = np.random.permutation(np.resize(levels, 8))
        for g in range(8):
            far = levels[np.abs(levels - a[p, g]) >= 10]
            a[p, g + 8] = far[np.random.randint(len(far))]
    return np.exp2(a.ravel()).repeat(32)


BF16 = ml_dtypes.bfloat16


def bf(x):
    return np.asarray(x, np.float32).astype(BF16)


def f64(x):
    return np.asarray(x).astype(np.float64)


B, S, D, H = 2, 64, 512, 1024
HEAD = H // 2


def rotate_every_two(x):
    x1 = x[..., ::2]
    x2 = x[..., 1::2]
    return np.stack((-x2, x1), axis=-1).reshape(x.shape)


def rope_table(seq_len):
    pos = np.arange(seq_len, dtype=np.float64)
    inv = 10000.0 ** (np.arange(0, HEAD, 2, dtype=np.float64) / HEAD)
    radians = pos[:, None] / inv
    sincos = np.stack((np.sin(radians), np.cos(radians)), axis=-1).reshape(seq_len, -1)
    return np.repeat(sincos, 2, axis=-1)


def setup_inputs():
    s = mx_kscale(D)
    u = np.repeat(mx_kscale(HEAD), 2)
    return {"hidden_states": bf(np.random.standard_normal((B, S, D)) * s),
            "Wq": bf(np.random.standard_normal((H, D)) / np.sqrt(D) / s * u[:, None]),
            "bq": bf(np.random.standard_normal(H) * 0.3 * u),
            "Wk": bf(np.random.standard_normal((H, D)) / np.sqrt(D) / s / u[:, None]),
            "bk": bf(np.random.standard_normal(H) * 0.3 / u)}


def reference(hidden_states, Wq, bq, Wk, bk):
    t = rope_table(hidden_states.shape[1])
    xq = mxq(f64(hidden_states), 2, "e4m3")
    q = (xq @ mxq(f64(Wq), 1, "e4m3").T) + f64(bq)
    k = (xq @ mxq(f64(Wk), 1, "e4m3").T) + f64(bk)
    q = q * t + rotate_every_two(q) * t
    k = k * t + rotate_every_two(k) * t
    return (mxq(q, 2, "e4m3") @ mxq(k, 2, "e4m3").transpose(0, 2, 1)) / np.sqrt(HEAD)

@@ -1,0 +1,266 @@
+import math
+from contextlib import ExitStack
+
+import concourse.mybir as mybir
+from concourse.masks import make_identity
+
+F32 = mybir.dt.float32
+BF16 = mybir.dt.bfloat16
+U32 = mybir.dt.uint32
+U8 = mybir.dt.uint8
+I32 = mybir.dt.int32
+FP8X4 = mybir.dt.float8_e4m3fn_x4
+ALU = mybir.AluOpType
+ACT = mybir.ActivationFunctionType
+
+P = 128
+PACK = 4
+K_PASS = P * PACK
+
+BATCH, SEQ, D_IN, D_OUT = 2, 64, 512, 1024
+TOKENS = BATCH * SEQ
+HEAD = D_OUT // 2
+F_PASSES = D_OUT // K_PASS
+SIDES = ("q", "k")
+CHUNKS = F_PASSES * len(SIDES)
+
+WARM_PASSES = 14
+LEAD = 3
+
+FLOPS = 2 * 2 * TOKENS * D_IN * D_OUT + 2 * BATCH * SEQ * SEQ * D_OUT
+
+ROUND_TO_INT = 12582912.0
+TWO_PI_HI = 6.28125
+TWO_PI_LO = 2.0 * math.pi - TWO_PI_HI
+
+
+def tile_ropeattention_pa_s_kernel(tc, hidden_states, Wq, bq, Wk, bk, out):
+    nc = tc.nc
+    weights = {"q": Wq, "k": Wk}
+    biases = {"q": bq, "k": bk}
+
+    with ExitStack() as ctx:
+        ctx.enter_context(tc.manual_schedule())
+        keep = ctx.enter_context(tc.tile_pool(name="keep", bufs=1))
+        transposed = ctx.enter_context(tc.psum_pool(name="transposed", bufs=4))
+        projected = ctx.enter_context(tc.psum_pool(name="projected", bufs=3))
+        scores = ctx.enter_context(tc.psum_pool(name="scores", bufs=1))
+
+        bias_rows = {}
+        for side in SIDES:
+            bias_rows[side] = keep.tile([P, F_PASSES, PACK], BF16, name="bias_rows_%s" % side)
+            nc.scalar.dma_start(
+                out=bias_rows[side][:],
+                in_=biases[side].rearrange("(c p t) -> p c t", p=P, t=PACK),
+            )
+        x_rows = keep.tile([P, D_IN], BF16)
+        nc.sync.dma_start(out=x_rows[:], in_=hidden_states.rearrange("b s d -> (b s) d"))
+        w_rows = keep.tile([P, CHUNKS, PACK, D_IN], BF16)
+        for i in range(CHUNKS):
+            chunk_rows = weights[SIDES[i % 2]][(i // 2) * K_PASS : (i // 2 + 1) * K_PASS, :].rearrange(
+                "(p t) d -> p t d", t=PACK
+            )
+            for h in range(2):
+                nc.sync.dma_start(out=w_rows[:, i, 2 * h : 2 * h + 2, :], in_=chunk_rows[:, 2 * h : 2 * h + 2, :])
+
+        score = scores.tile([P, TOKENS], F32)
+        idle_grouped = keep.tile([P, TOKENS, PACK], BF16, align_bytes=64)
+        idle_codes = keep.tile([P, TOKENS], U32, align_bytes=64)
+        idle_scales = keep.tile([P, TOKENS], U8, align_bytes=64)
+        nc.vector.memset(idle_grouped[:].bitcast(I32), 0)
+        nc.vector.quantize_mx(
+            out=idle_codes[:].bitcast(FP8X4),
+            scales=idle_scales[:],
+            in_=idle_grouped[:].rearrange("p n t -> p (n t)"),
+        )
+
+        for n in range(WARM_PASSES):
+            nc.tensor.matmul_mx(
+                out=score[:],
+                lhsT=idle_codes[:].bitcast(FP8X4),
+                lhsT_scale=idle_scales[:],
+                rhs=idle_codes[:].bitcast(FP8X4),
+                rhs_scale=idle_scales[:],
+                start=True,
+                stop=True,
+            )
+
+        ten_thousand = keep.tile([P, F_PASSES], F32)
+        nc.vector.memset(ten_thousand[:], 10000.0)
+        exponent = keep.tile([P, F_PASSES], F32)
+        nc.gpsimd.iota(
+            exponent[:],
+            pattern=[[P, F_PASSES]],
+            base=0,
+            channel_multiplier=1,
+            allow_small_or_imprecise_dtypes=True,
+        )
+        nc.gpsimd.tensor_scalar(
+            out=exponent[:], in0=exponent[:], scalar1=-2.0 / HEAD, scalar2=0.0, op0=ALU.mult, op1=ALU.add
+        )
+        frequency = keep.tile([P, F_PASSES], F32)
+        nc.gpsimd.tensor_tensor(out=frequency[:], in0=ten_thousand[:], in1=exponent[:], op=ALU.pow)
+        position = keep.tile([P, SEQ], F32)
+        nc.gpsimd.iota(
+            position[:], pattern=[[1, SEQ]], base=0, channel_multiplier=0, allow_small_or_imprecise_dtypes=True
+        )
+        identity = keep.tile([P, P], F32)
+        make_identity(nc, identity[:])
+
+        bias_rot = {}
+        for side in SIDES:
+            pairs = bias_rows[side][:].rearrange("p c (h e) -> p (c h) e", e=2)
+            bias_rot[side] = keep.tile([P, F_PASSES, PACK], F32, name="bias_rot_%s" % side)
+            rotated = bias_rot[side][:].rearrange("p c (h e) -> p (c h) e", e=2)
+            nc.gpsimd.tensor_tensor(out=rotated[:, :, 0], in0=pairs[:, :, 0], in1=pairs[:, :, 1], op=ALU.subtract)
+            nc.gpsimd.tensor_tensor(out=rotated[:, :, 1], in0=pairs[:, :, 0], in1=pairs[:, :, 1], op=ALU.add)
+
+        angle = keep.tile([P, F_PASSES, 2, SEQ], F32)
+        for c in range(F_PASSES):
+            for h in range(2):
+                nc.vector.tensor_scalar(
+                    out=angle[:, c, h, :],
+                    in0=position[:],
+                    scalar1=frequency[:, c : c + 1],
+                    scalar2=h * math.pi / 2.0,
+                    op0=ALU.mult,
+                    op1=ALU.add,
+                )
+        flat = "p c h s -> p (c h s)"
+        turns = keep.tile([P, F_PASSES, 2, SEQ], F32)
+        nc.vector.tensor_scalar(
+            out=turns[:], in0=angle[:], scalar1=1.0 / (2.0 * math.pi), scalar2=ROUND_TO_INT, op0=ALU.mult, op1=ALU.add
+        )
+        nc.vector.tensor_scalar(out=turns[:], in0=turns[:], scalar1=ROUND_TO_INT, scalar2=None, op0=ALU.subtract)
+        reduced = keep.tile([P, F_PASSES, 2, SEQ], F32)
+        nc.vector.scalar_tensor_tensor(
+            out=reduced[:].rearrange(flat),
+            in0=turns[:].rearrange(flat),
+            scalar=-TWO_PI_HI,
+            in1=angle[:].rearrange(flat),
+            op0=ALU.mult,
+            op1=ALU.add,
+        )
+        nc.vector.scalar_tensor_tensor(
+            out=reduced[:].rearrange(flat),
+            in0=turns[:].rearrange(flat),
+            scalar=-TWO_PI_LO,
+            in1=reduced[:].rearrange(flat),
+            op0=ALU.mult,
+            op1=ALU.add,
+        )
+
+        x_words = x_rows[:].bitcast(F32)
+        xT = transposed.tile([P, 2, TOKENS], F32, tag="bank")
+        for u in range(2):
+            nc.tensor.transpose(xT[:, u, :], x_words[:, u :: 2], identity[:])
+        x_grouped = keep.tile([P, 3, TOKENS, PACK], BF16, align_bytes=64)
+        nc.vector.tensor_copy(
+            out=x_grouped[:, 1:3].bitcast(F32),
+            in_=xT[:].rearrange("p u n -> p n u").unsqueeze(1).to_broadcast([P, 2, TOKENS, 2]),
+        )
+        table = keep.tile([P, F_PASSES, 2, SEQ], F32)
+        nc.scalar.activation(out=table[:], in_=reduced[:], func=ACT.Sin)
+        nc.vector.tensor_scalar(
+            out=x_grouped[:, 0], in0=x_grouped[:, 1], scalar1=-1.0, scalar2=None, op0=ALU.mult
+        )
+        x_codes = keep.tile([P, 3 * TOKENS], U32, align_bytes=64)
+        x_scales = keep.tile([P, 3 * TOKENS], U8, align_bytes=64)
+        minus_plus = slice(0, 2 * TOKENS)
+        plus_plus = slice(TOKENS, 3 * TOKENS)
+        last_copy = slice(2 * TOKENS, 3 * TOKENS)
+        nc.vector.quantize_mx(
+            out=x_codes[:, minus_plus].bitcast(FP8X4),
+            scales=x_scales[:, minus_plus],
+            in_=x_grouped[:, 0:2].rearrange("p a n t -> p (a n t)"),
+        )
+        nc.vector.quantize_mx(
+            out=x_codes[:, last_copy].bitcast(FP8X4),
+            scales=x_scales[:, last_copy],
+            in_=x_grouped[:, 2].rearrange("p n t -> p (n t)"),
+        )
+
+        w_words = w_rows[:].bitcast(F32)
+        w_grouped = keep.tile([P, CHUNKS, PACK, P, PACK], BF16, align_bytes=64)
+        w_codes = keep.tile([P, CHUNKS, PACK, P], U32, align_bytes=64)
+        w_scales = keep.tile([P, CHUNKS, PACK, P], U8, align_bytes=64)
+        rot_planes = keep.tile([P, CHUNKS, PACK, TOKENS], BF16)
+        rot_grouped = keep.tile([P, CHUNKS, TOKENS, PACK], BF16, align_bytes=64)
+        rot_codes = keep.tile([P, CHUNKS, TOKENS], U32, align_bytes=64)
+        rot_scales = keep.tile([P, CHUNKS, TOKENS], U8, align_bytes=64)
+
+        def quantise_weights(i):
+            for h in range(2):
+                rows = slice(2 * h, 2 * h + 2)
+                wT = transposed.tile([P, 2, 2, P], F32, tag="bank")
+                for e in range(2):
+                    for u in range(2):
+                        nc.tensor.transpose(
+                            wT[:, e, u, :], w_words[:, i, 2 * h + e, u :: 2], identity[:]
+                        )
+                nc.scalar.copy(out=w_grouped[:, i, rows].bitcast(F32), in_=wT[:].rearrange("p e u m -> p e m u"))
+                nc.vector.quantize_mx(
+                    out=w_codes[:, i, rows].rearrange("p e m -> p (e m)").bitcast(FP8X4),
+                    scales=w_scales[:, i, rows].rearrange("p e m -> p (e m)"),
+                    in_=w_grouped[:, i, rows].rearrange("p e m t -> p (e m t)"),
+                )
+
+        def project_and_rotate(i):
+            y = projected.tile([P, PACK, TOKENS], F32)
+            for t in range(PACK):
+                moving = plus_plus if t % 2 == 0 else minus_plus
+                nc.tensor.matmul_mx(
+                    out=y[:, t - t % 2 : t - t % 2 + 2, :].rearrange("p e n -> p (e n)"),
+                    lhsT=w_codes[:, i, t, :].bitcast(FP8X4),
+                    lhsT_scale=w_scales[:, i, t, :],
+                    rhs=x_codes[:, moving].bitcast(FP8X4),
+                    rhs_scale=x_scales[:, moving],
+                    start=(t % 2 == 0),
+                    stop=(t % 2 == 1),
+                )
+            for t in range(PACK):
+                nc.vector.scalar_tensor_tensor(
+                    out=rot_planes[:, i, t, :].rearrange("p (b s) -> p b s", b=BATCH),
+                    in0=y[:, t, :].rearrange("p (b s) -> p b s", b=BATCH),
+                    scalar=bias_rot[SIDES[i % 2]][:, i // 2, t : t + 1],
+                    in1=table[:, i // 2, t // 2, :].unsqueeze(1).to_broadcast([P, BATCH, SEQ]),
+                    op0=ALU.add,
+                    op1=ALU.mult,
+                )
+
+        def quantise_rotated(i):
+            regroup = nc.vector.tensor_copy if i == CHUNKS - 1 else nc.scalar.copy
+            regroup(out=rot_grouped[:, i], in_=rot_planes[:, i].rearrange("p t n -> p n t"))
+            nc.vector.quantize_mx(
+                out=rot_codes[:, i, :].bitcast(FP8X4),
+                scales=rot_scales[:, i, :],
+                in_=rot_grouped[:, i].rearrange("p n t -> p (n t)"),
+            )
+
+        for i in range(LEAD):
+            quantise_weights(i)
+        for i in range(CHUNKS):
+            project_and_rotate(i)
+            if i >= 1:
+                quantise_rotated(i - 1)
+            if i + LEAD < CHUNKS:
+                quantise_weights(i + LEAD)
+        quantise_rotated(CHUNKS - 1)
+
+        for c in range(F_PASSES):
+            nc.tensor.matmul_mx(
+                out=score[:],
+                lhsT=rot_codes[:, 2 * c, :].bitcast(FP8X4),
+                lhsT_scale=rot_scales[:, 2 * c, :],
+                rhs=rot_codes[:, 2 * c + 1, :].bitcast(FP8X4),
+                rhs_scale=rot_scales[:, 2 * c + 1, :],
+                start=(c == 0),
+                stop=(c == F_PASSES - 1),
+            )
+
+        scaled = keep.tile([P, SEQ], F32)
+        nc.vector.tensor_scalar(
+            out=scaled[0:SEQ, :], in0=score[0:SEQ, 0:SEQ], scalar1=1.0 / math.sqrt(HEAD), scalar2=None, op0=ALU.mult
+        )
+        nc.scalar.mul(out=scaled[SEQ:P, :], in_=score[SEQ:P, SEQ:P], mul=1.0 / math.sqrt(HEAD))
+        nc.sync.dma_start(out=out.rearrange("b s j -> (b s) j"), in_=scaled[:])

@@ -30,8 +30,7 @@ LEAD = 3
 FLOPS = 2 * 2 * TOKENS * D_IN * D_OUT + 2 * BATCH * SEQ * SEQ * D_OUT
 
 ROUND_TO_INT = 12582912.0
-TWO_PI_HI = 6.28125
-TWO_PI_LO = 2.0 * math.pi - TWO_PI_HI
+TWO_PI = 2.0 * math.pi
 
 
 def tile_ropeattention_pa_s_kernel(tc, hidden_states, Wq, bq, Wk, bk, out):
@@ -46,13 +45,6 @@ def tile_ropeattention_pa_s_kernel(tc, hidden_states, Wq, bq, Wk, bk, out):
         projected = ctx.enter_context(tc.psum_pool(name="projected", bufs=3))
         scores = ctx.enter_context(tc.psum_pool(name="scores", bufs=1))
 
-        bias_rows = {}
-        for side in SIDES:
-            bias_rows[side] = keep.tile([P, F_PASSES, PACK], BF16, name="bias_rows_%s" % side)
-            nc.scalar.dma_start(
-                out=bias_rows[side][:],
-                in_=biases[side].rearrange("(c p t) -> p c t", p=P, t=PACK),
-            )
         x_rows = keep.tile([P, D_IN], BF16)
         nc.sync.dma_start(out=x_rows[:], in_=hidden_states.rearrange("b s d -> (b s) d"))
         w_rows = keep.tile([P, CHUNKS, PACK, D_IN], BF16)
@@ -64,15 +56,19 @@ def tile_ropeattention_pa_s_kernel(tc, hidden_states, Wq, bq, Wk, bk, out):
                 nc.sync.dma_start(out=w_rows[:, i, 2 * h : 2 * h + 2, :], in_=chunk_rows[:, 2 * h : 2 * h + 2, :])
 
         score = scores.tile([P, TOKENS], F32)
-        idle_grouped = keep.tile([P, TOKENS, PACK], BF16, align_bytes=64)
+        ten_thousand = keep.tile([P, F_PASSES], F32)
+        nc.vector.memset(ten_thousand[:], 10000.0)
+        zero_rows = keep.tile([P, K_PASS], BF16, align_bytes=64)
         idle_codes = keep.tile([P, TOKENS], U32, align_bytes=64)
         idle_scales = keep.tile([P, TOKENS], U8, align_bytes=64)
-        nc.vector.memset(idle_grouped[:].bitcast(I32), 0)
-        nc.vector.quantize_mx(
-            out=idle_codes[:].bitcast(FP8X4),
-            scales=idle_scales[:],
-            in_=idle_grouped[:].rearrange("p n t -> p (n t)"),
-        )
+        nc.vector.memset(zero_rows[:].bitcast(I32), 0)
+        nc.vector.quantize_mx(out=idle_codes[:].bitcast(FP8X4), scales=idle_scales[:], in_=zero_rows[:])
+
+        for n, side in enumerate(SIDES):
+            nc.scalar.dma_start(
+                out=zero_rows[F_PASSES * n : F_PASSES * (n + 1), :],
+                in_=biases[side].rearrange("(c k) -> c k", c=F_PASSES),
+            )
 
         for n in range(WARM_PASSES):
             nc.tensor.matmul_mx(
@@ -85,8 +81,6 @@ def tile_ropeattention_pa_s_kernel(tc, hidden_states, Wq, bq, Wk, bk, out):
                 stop=True,
             )
 
-        ten_thousand = keep.tile([P, F_PASSES], F32)
-        nc.vector.memset(ten_thousand[:], 10000.0)
         exponent = keep.tile([P, F_PASSES], F32)
         nc.gpsimd.iota(
             exponent[:],
@@ -98,86 +92,72 @@ def tile_ropeattention_pa_s_kernel(tc, hidden_states, Wq, bq, Wk, bk, out):
         nc.gpsimd.tensor_scalar(
             out=exponent[:], in0=exponent[:], scalar1=-2.0 / HEAD, scalar2=0.0, op0=ALU.mult, op1=ALU.add
         )
-        frequency = keep.tile([P, F_PASSES], F32)
-        nc.gpsimd.tensor_tensor(out=frequency[:], in0=ten_thousand[:], in1=exponent[:], op=ALU.pow)
         position = keep.tile([P, SEQ], F32)
         nc.gpsimd.iota(
             position[:], pattern=[[1, SEQ]], base=0, channel_multiplier=0, allow_small_or_imprecise_dtypes=True
         )
+        frequency = keep.tile([P, F_PASSES], F32)
+        nc.gpsimd.tensor_tensor(out=frequency[:], in0=ten_thousand[:], in1=exponent[:], op=ALU.pow)
         identity = keep.tile([P, P], F32)
         make_identity(nc, identity[:])
 
-        bias_rot = {}
-        for side in SIDES:
-            pairs = bias_rows[side][:].rearrange("p c (h e) -> p (c h) e", e=2)
-            bias_rot[side] = keep.tile([P, F_PASSES, PACK], F32, name="bias_rot_%s" % side)
-            rotated = bias_rot[side][:].rearrange("p c (h e) -> p (c h) e", e=2)
-            nc.gpsimd.tensor_tensor(out=rotated[:, :, 0], in0=pairs[:, :, 0], in1=pairs[:, :, 1], op=ALU.subtract)
-            nc.gpsimd.tensor_tensor(out=rotated[:, :, 1], in0=pairs[:, :, 0], in1=pairs[:, :, 1], op=ALU.add)
-
+        position_turns = keep.tile([P, SEQ], F32)
+        nc.vector.tensor_scalar(
+            out=position_turns[:], in0=position[:], scalar1=1.0 / TWO_PI, scalar2=None, op0=ALU.mult
+        )
         angle = keep.tile([P, F_PASSES, 2, SEQ], F32)
         for c in range(F_PASSES):
             for h in range(2):
                 nc.vector.tensor_scalar(
                     out=angle[:, c, h, :],
-                    in0=position[:],
+                    in0=position_turns[:],
                     scalar1=frequency[:, c : c + 1],
-                    scalar2=h * math.pi / 2.0,
+                    scalar2=h * 0.25,
                     op0=ALU.mult,
                     op1=ALU.add,
                 )
         flat = "p c h s -> p (c h s)"
         turns = keep.tile([P, F_PASSES, 2, SEQ], F32)
         nc.vector.tensor_scalar(
-            out=turns[:], in0=angle[:], scalar1=1.0 / (2.0 * math.pi), scalar2=ROUND_TO_INT, op0=ALU.mult, op1=ALU.add
+            out=turns[:], in0=angle[:], scalar1=ROUND_TO_INT, scalar2=None, op0=ALU.add
         )
-        nc.vector.tensor_scalar(out=turns[:], in0=turns[:], scalar1=ROUND_TO_INT, scalar2=None, op0=ALU.subtract)
-        reduced = keep.tile([P, F_PASSES, 2, SEQ], F32)
+        minus_rest = keep.tile([P, F_PASSES, 2, SEQ], F32)
         nc.vector.scalar_tensor_tensor(
-            out=reduced[:].rearrange(flat),
+            out=minus_rest[:].rearrange(flat),
             in0=turns[:].rearrange(flat),
-            scalar=-TWO_PI_HI,
+            scalar=ROUND_TO_INT,
             in1=angle[:].rearrange(flat),
-            op0=ALU.mult,
-            op1=ALU.add,
+            op0=ALU.subtract,
+            op1=ALU.subtract,
         )
-        nc.vector.scalar_tensor_tensor(
-            out=reduced[:].rearrange(flat),
-            in0=turns[:].rearrange(flat),
-            scalar=-TWO_PI_LO,
-            in1=reduced[:].rearrange(flat),
-            op0=ALU.mult,
-            op1=ALU.add,
-        )
+        table = keep.tile([P, F_PASSES, 2, SEQ], F32)
+        nc.scalar.activation(out=table[:], in_=minus_rest[:], func=ACT.Sin, scale=-TWO_PI)
 
         x_words = x_rows[:].bitcast(F32)
         xT = transposed.tile([P, 2, TOKENS], F32, tag="bank")
         for u in range(2):
             nc.tensor.transpose(xT[:, u, :], x_words[:, u :: 2], identity[:])
-        x_grouped = keep.tile([P, 3, TOKENS, PACK], BF16, align_bytes=64)
+        x_grouped = keep.tile([P, 2, TOKENS, PACK], BF16, align_bytes=64)
         nc.vector.tensor_copy(
-            out=x_grouped[:, 1:3].bitcast(F32),
-            in_=xT[:].rearrange("p u n -> p n u").unsqueeze(1).to_broadcast([P, 2, TOKENS, 2]),
-        )
-        table = keep.tile([P, F_PASSES, 2, SEQ], F32)
-        nc.scalar.activation(out=table[:], in_=reduced[:], func=ACT.Sin)
-        nc.vector.tensor_scalar(
-            out=x_grouped[:, 0], in0=x_grouped[:, 1], scalar1=-1.0, scalar2=None, op0=ALU.mult
+            out=x_grouped[:, 1].bitcast(F32), in_=xT[:].rearrange("p u n -> p n u")
         )
         x_codes = keep.tile([P, 3 * TOKENS], U32, align_bytes=64)
         x_scales = keep.tile([P, 3 * TOKENS], U8, align_bytes=64)
         minus_plus = slice(0, 2 * TOKENS)
         plus_plus = slice(TOKENS, 3 * TOKENS)
         last_copy = slice(2 * TOKENS, 3 * TOKENS)
-        nc.vector.quantize_mx(
-            out=x_codes[:, minus_plus].bitcast(FP8X4),
-            scales=x_scales[:, minus_plus],
-            in_=x_grouped[:, 0:2].rearrange("p a n t -> p (a n t)"),
+        nc.vector.tensor_scalar(
+            out=x_grouped[:, 0], in0=x_grouped[:, 1], scalar1=-1.0, scalar2=None, op0=ALU.mult
         )
         nc.vector.quantize_mx(
             out=x_codes[:, last_copy].bitcast(FP8X4),
             scales=x_scales[:, last_copy],
-            in_=x_grouped[:, 2].rearrange("p n t -> p (n t)"),
+            in_=x_grouped[:, 1].rearrange("p n t -> p (n t)"),
+        )
+        nc.vector.quantize_mx(
+            out=x_codes[:, minus_plus].bitcast(FP8X4),
+            scales=x_scales[:, minus_plus],
+            in_=x_grouped[:].rearrange("p a n t -> p (a n t)"),
         )
 
         w_words = w_rows[:].bitcast(F32)
@@ -205,6 +185,20 @@ def tile_ropeattention_pa_s_kernel(tc, hidden_states, Wq, bq, Wk, bk, out):
                     in_=w_grouped[:, i, rows].rearrange("p e m t -> p (e m t)"),
                 )
 
+        bias_columns = keep.tile([P, CHUNKS, PACK], BF16)
+        bias_rot = keep.tile([P, CHUNKS, PACK], F32)
+
+        def turn_biases():
+            bias_words = zero_rows[:].bitcast(F32)
+            bT = transposed.tile([P, 2, P], F32, tag="bank")
+            for u in range(2):
+                nc.tensor.transpose(bT[:, u, :], bias_words[:, u::2], identity[:])
+            nc.scalar.copy(out=bias_columns[:].bitcast(F32), in_=bT[:, :, 0:CHUNKS].rearrange("p u r -> p r u"))
+            pairs = bias_columns[:].rearrange("p r (h e) -> p (r h) e", e=2)
+            rotated = bias_rot[:].rearrange("p r (h e) -> p (r h) e", e=2)
+            nc.gpsimd.tensor_tensor(out=rotated[:, :, 0], in0=pairs[:, :, 0], in1=pairs[:, :, 1], op=ALU.subtract)
+            nc.gpsimd.tensor_tensor(out=rotated[:, :, 1], in0=pairs[:, :, 0], in1=pairs[:, :, 1], op=ALU.add)
+
         def project_and_rotate(i):
             y = projected.tile([P, PACK, TOKENS], F32)
             for t in range(PACK):
@@ -222,7 +216,7 @@ def tile_ropeattention_pa_s_kernel(tc, hidden_states, Wq, bq, Wk, bk, out):
                 nc.vector.scalar_tensor_tensor(
                     out=rot_planes[:, i, t, :].rearrange("p (b s) -> p b s", b=BATCH),
                     in0=y[:, t, :].rearrange("p (b s) -> p b s", b=BATCH),
-                    scalar=bias_rot[SIDES[i % 2]][:, i // 2, t : t + 1],
+                    scalar=bias_rot[:, F_PASSES * (i % 2) + i // 2, t : t + 1],
                     in1=table[:, i // 2, t // 2, :].unsqueeze(1).to_broadcast([P, BATCH, SEQ]),
                     op0=ALU.add,
                     op1=ALU.mult,
@@ -239,6 +233,8 @@ def tile_ropeattention_pa_s_kernel(tc, hidden_states, Wq, bq, Wk, bk, out):
 
         for i in range(LEAD):
             quantise_weights(i)
+            if i == 0:
+                turn_biases()
         for i in range(CHUNKS):
             project_and_rotate(i)
             if i >= 1:
@@ -262,5 +258,7 @@ def tile_ropeattention_pa_s_kernel(tc, hidden_states, Wq, bq, Wk, bk, out):
         nc.vector.tensor_scalar(
             out=scaled[0:SEQ, :], in0=score[0:SEQ, 0:SEQ], scalar1=1.0 / math.sqrt(HEAD), scalar2=None, op0=ALU.mult
         )
-        nc.scalar.mul(out=scaled[SEQ:P, :], in_=score[SEQ:P, SEQ:P], mul=1.0 / math.sqrt(HEAD))
+        nc.vector.tensor_scalar(
+            out=scaled[SEQ:P, :], in0=score[SEQ:P, SEQ:P], scalar1=1.0 / math.sqrt(HEAD), scalar2=None, op0=ALU.mult
+        )
         nc.sync.dma_start(out=out.rearrange("b s j -> (b s) j"), in_=scaled[:])

@@ -45,8 +45,17 @@ def tile_ropeattention_pa_s_kernel(tc, hidden_states, Wq, bq, Wk, bk, out):
         projected = ctx.enter_context(tc.psum_pool(name="projected", bufs=3))
         scores = ctx.enter_context(tc.psum_pool(name="scores", bufs=1))
 
+        ten_thousand = keep.tile([P, F_PASSES], F32)
+        nc.vector.memset(ten_thousand[:], 10000.0)
+        bias_rows = keep.tile([P, K_PASS], BF16)
+        nc.vector.memset(bias_rows[:].bitcast(I32), 0)
         x_rows = keep.tile([P, D_IN], BF16)
         nc.sync.dma_start(out=x_rows[:], in_=hidden_states.rearrange("b s d -> (b s) d"))
+        for n, side in enumerate(SIDES):
+            nc.sync.dma_start(
+                out=bias_rows[F_PASSES * n : F_PASSES * (n + 1), :],
+                in_=biases[side].rearrange("(c k) -> c k", c=F_PASSES),
+            )
         w_rows = keep.tile([P, CHUNKS, PACK, D_IN], BF16)
         for i in range(CHUNKS):
             chunk_rows = weights[SIDES[i % 2]][(i // 2) * K_PASS : (i // 2 + 1) * K_PASS, :].rearrange(
@@ -56,19 +65,11 @@ def tile_ropeattention_pa_s_kernel(tc, hidden_states, Wq, bq, Wk, bk, out):
                 nc.sync.dma_start(out=w_rows[:, i, 2 * h : 2 * h + 2, :], in_=chunk_rows[:, 2 * h : 2 * h + 2, :])
 
         score = scores.tile([P, TOKENS], F32)
-        ten_thousand = keep.tile([P, F_PASSES], F32)
-        nc.vector.memset(ten_thousand[:], 10000.0)
         zero_rows = keep.tile([P, K_PASS], BF16, align_bytes=64)
         idle_codes = keep.tile([P, TOKENS], U32, align_bytes=64)
         idle_scales = keep.tile([P, TOKENS], U8, align_bytes=64)
         nc.vector.memset(zero_rows[:].bitcast(I32), 0)
         nc.vector.quantize_mx(out=idle_codes[:].bitcast(FP8X4), scales=idle_scales[:], in_=zero_rows[:])
-
-        for n, side in enumerate(SIDES):
-            nc.scalar.dma_start(
-                out=zero_rows[F_PASSES * n : F_PASSES * (n + 1), :],
-                in_=biases[side].rearrange("(c k) -> c k", c=F_PASSES),
-            )
 
         for n in range(WARM_PASSES):
             nc.tensor.matmul_mx(
@@ -189,7 +190,7 @@ def tile_ropeattention_pa_s_kernel(tc, hidden_states, Wq, bq, Wk, bk, out):
         bias_rot = keep.tile([P, CHUNKS, PACK], F32)
 
         def turn_biases():
-            bias_words = zero_rows[:].bitcast(F32)
+            bias_words = bias_rows[:].bitcast(F32)
             bT = transposed.tile([P, 2, P], F32, tag="bank")
             for u in range(2):
                 nc.tensor.transpose(bT[:, u, :], bias_words[:, u::2], identity[:])

@@ -25,7 +25,7 @@ SIDES = ("q", "k")
 CHUNKS = F_PASSES * len(SIDES)
 
 WARM_PASSES = 14
-LEAD = 3
+LEAD = 4
 
 FLOPS = 2 * 2 * TOKENS * D_IN * D_OUT + 2 * BATCH * SEQ * SEQ * D_OUT
 
@@ -131,8 +131,14 @@ def tile_ropeattention_pa_s_kernel(tc, hidden_states, Wq, bq, Wk, bk, out):
             op0=ALU.subtract,
             op1=ALU.subtract,
         )
-        table = keep.tile([P, F_PASSES, 2, SEQ], F32)
-        nc.scalar.activation(out=table[:], in_=minus_rest[:], func=ACT.Sin, scale=-TWO_PI)
+        table = keep.tile([P, F_PASSES, SEQ, PACK], F32)
+        for c in range(F_PASSES):
+            nc.scalar.activation(
+                out=table[:, c].rearrange("p s (h e) -> p s h e", e=2),
+                in_=minus_rest[:, c].rearrange("p h s -> p s h").unsqueeze(3).to_broadcast([P, SEQ, 2, 2]),
+                func=ACT.Sin,
+                scale=-TWO_PI,
+            )
 
         x_words = x_rows[:].bitcast(F32)
         xT = transposed.tile([P, 2, TOKENS], F32, tag="bank")
@@ -165,21 +171,20 @@ def tile_ropeattention_pa_s_kernel(tc, hidden_states, Wq, bq, Wk, bk, out):
         w_grouped = keep.tile([P, CHUNKS, PACK, P, PACK], BF16, align_bytes=64)
         w_codes = keep.tile([P, CHUNKS, PACK, P], U32, align_bytes=64)
         w_scales = keep.tile([P, CHUNKS, PACK, P], U8, align_bytes=64)
-        rot_planes = keep.tile([P, CHUNKS, PACK, TOKENS], BF16)
+        biased = keep.tile([P, CHUNKS, PACK, TOKENS], F32)
         rot_grouped = keep.tile([P, CHUNKS, TOKENS, PACK], BF16, align_bytes=64)
         rot_codes = keep.tile([P, CHUNKS, TOKENS], U32, align_bytes=64)
         rot_scales = keep.tile([P, CHUNKS, TOKENS], U8, align_bytes=64)
 
-        def quantise_weights(i):
-            for h in range(2):
-                rows = slice(2 * h, 2 * h + 2)
+        def quantise_weights(i, copies):
+            halves = [slice(2 * h, 2 * h + 2) for h in range(2)]
+            for rows, copy in zip(halves, copies):
                 wT = transposed.tile([P, 2, 2, P], F32, tag="bank")
                 for e in range(2):
                     for u in range(2):
-                        nc.tensor.transpose(
-                            wT[:, e, u, :], w_words[:, i, 2 * h + e, u :: 2], identity[:]
-                        )
-                nc.scalar.copy(out=w_grouped[:, i, rows].bitcast(F32), in_=wT[:].rearrange("p e u m -> p e m u"))
+                        nc.tensor.transpose(wT[:, e, u, :], w_words[:, i, rows.start + e, u::2], identity[:])
+                copy(out=w_grouped[:, i, rows].bitcast(F32), in_=wT[:].rearrange("p e u m -> p e m u"))
+            for rows in halves:
                 nc.vector.quantize_mx(
                     out=w_codes[:, i, rows].rearrange("p e m -> p (e m)").bitcast(FP8X4),
                     scales=w_scales[:, i, rows].rearrange("p e m -> p (e m)"),
@@ -214,26 +219,30 @@ def tile_ropeattention_pa_s_kernel(tc, hidden_states, Wq, bq, Wk, bk, out):
                     stop=(t % 2 == 1),
                 )
             for t in range(PACK):
-                nc.vector.scalar_tensor_tensor(
-                    out=rot_planes[:, i, t, :].rearrange("p (b s) -> p b s", b=BATCH),
-                    in0=y[:, t, :].rearrange("p (b s) -> p b s", b=BATCH),
-                    scalar=bias_rot[:, F_PASSES * (i % 2) + i // 2, t : t + 1],
-                    in1=table[:, i // 2, t // 2, :].unsqueeze(1).to_broadcast([P, BATCH, SEQ]),
-                    op0=ALU.add,
-                    op1=ALU.mult,
+                nc.scalar.activation(
+                    out=biased[:, i, t, :],
+                    in_=y[:, t, :],
+                    func=ACT.Identity,
+                    bias=bias_rot[:, F_PASSES * (i % 2) + i // 2, t : t + 1],
                 )
+            nc.vector.tensor_tensor(
+                out=rot_grouped[:, i].rearrange("p (b s) t -> p b s t", b=BATCH),
+                in0=biased[:, i].rearrange("p t (b s) -> p b s t", b=BATCH),
+                in1=table[:, i // 2].unsqueeze(1).to_broadcast([P, BATCH, SEQ, PACK]),
+                op=ALU.mult,
+            )
 
         def quantise_rotated(i):
-            regroup = nc.vector.tensor_copy if i == CHUNKS - 1 else nc.scalar.copy
-            regroup(out=rot_grouped[:, i], in_=rot_planes[:, i].rearrange("p t n -> p n t"))
             nc.vector.quantize_mx(
                 out=rot_codes[:, i, :].bitcast(FP8X4),
                 scales=rot_scales[:, i, :],
                 in_=rot_grouped[:, i].rearrange("p n t -> p (n t)"),
             )
 
+        on_scalar = (nc.scalar.copy, nc.scalar.copy)
+        on_both = (nc.scalar.copy, nc.vector.tensor_copy)
         for i in range(LEAD):
-            quantise_weights(i)
+            quantise_weights(i, on_both if i >= 2 else on_scalar)
             if i == 0:
                 turn_biases()
         for i in range(CHUNKS):
@@ -241,7 +250,7 @@ def tile_ropeattention_pa_s_kernel(tc, hidden_states, Wq, bq, Wk, bk, out):
             if i >= 1:
                 quantise_rotated(i - 1)
             if i + LEAD < CHUNKS:
-                quantise_weights(i + LEAD)
+                quantise_weights(i + LEAD, on_scalar)
         quantise_rotated(CHUNKS - 1)
 
         for c in range(F_PASSES):

@@ -24,8 +24,8 @@ F_PASSES = D_OUT // K_PASS
 SIDES = ("q", "k")
 CHUNKS = F_PASSES * len(SIDES)
 
-WARM_PASSES = 14
-LEAD = 4
+RUN = 4
+WARM_PASSES = 12
 
 FLOPS = 2 * 2 * TOKENS * D_IN * D_OUT + 2 * BATCH * SEQ * SEQ * D_OUT
 
@@ -47,29 +47,14 @@ def tile_ropeattention_pa_s_kernel(tc, hidden_states, Wq, bq, Wk, bk, out):
 
         ten_thousand = keep.tile([P, F_PASSES], F32)
         nc.vector.memset(ten_thousand[:], 10000.0)
-        bias_rows = keep.tile([P, K_PASS], BF16)
-        nc.vector.memset(bias_rows[:].bitcast(I32), 0)
-        x_rows = keep.tile([P, D_IN], BF16)
-        nc.sync.dma_start(out=x_rows[:], in_=hidden_states.rearrange("b s d -> (b s) d"))
-        for n, side in enumerate(SIDES):
-            nc.sync.dma_start(
-                out=bias_rows[F_PASSES * n : F_PASSES * (n + 1), :],
-                in_=biases[side].rearrange("(c k) -> c k", c=F_PASSES),
-            )
-        w_rows = keep.tile([P, CHUNKS, PACK, D_IN], BF16)
-        for i in range(CHUNKS):
-            chunk_rows = weights[SIDES[i % 2]][(i // 2) * K_PASS : (i // 2 + 1) * K_PASS, :].rearrange(
-                "(p t) d -> p t d", t=PACK
-            )
-            for h in range(2):
-                nc.sync.dma_start(out=w_rows[:, i, 2 * h : 2 * h + 2, :], in_=chunk_rows[:, 2 * h : 2 * h + 2, :])
-
         score = scores.tile([P, TOKENS], F32)
         zero_rows = keep.tile([P, K_PASS], BF16, align_bytes=64)
         idle_codes = keep.tile([P, TOKENS], U32, align_bytes=64)
         idle_scales = keep.tile([P, TOKENS], U8, align_bytes=64)
         nc.vector.memset(zero_rows[:].bitcast(I32), 0)
         nc.vector.quantize_mx(out=idle_codes[:].bitcast(FP8X4), scales=idle_scales[:], in_=zero_rows[:])
+        bias_rows = keep.tile([P, K_PASS], BF16)
+        nc.vector.memset(bias_rows[:].bitcast(I32), 0)
 
         for n in range(WARM_PASSES):
             nc.tensor.matmul_mx(
@@ -81,6 +66,23 @@ def tile_ropeattention_pa_s_kernel(tc, hidden_states, Wq, bq, Wk, bk, out):
                 start=True,
                 stop=True,
             )
+
+        x_rows = keep.tile([P, D_IN], BF16)
+        w_rows = keep.tile([P, CHUNKS, PACK, D_IN], BF16)
+        for i in range(CHUNKS):
+            chunk_rows = weights[SIDES[i % 2]][(i // 2) * K_PASS : (i // 2 + 1) * K_PASS, :].rearrange(
+                "(p t) d -> p t d", t=PACK
+            )
+            for h in range(2):
+                nc.sync.dma_start(out=w_rows[:, i, 2 * h : 2 * h + 2, :], in_=chunk_rows[:, 2 * h : 2 * h + 2, :])
+            if i == 0:
+                nc.sync.dma_start(out=x_rows[:], in_=hidden_states.rearrange("b s d -> (b s) d"))
+            if i == 1:
+                for n, side in enumerate(SIDES):
+                    nc.sync.dma_start(
+                        out=bias_rows[F_PASSES * n : F_PASSES * (n + 1), :],
+                        in_=biases[side].rearrange("(c k) -> c k", c=F_PASSES),
+                    )
 
         exponent = keep.tile([P, F_PASSES], F32)
         nc.gpsimd.iota(
@@ -117,55 +119,64 @@ def tile_ropeattention_pa_s_kernel(tc, hidden_states, Wq, bq, Wk, bk, out):
                     op0=ALU.mult,
                     op1=ALU.add,
                 )
-        flat = "p c h s -> p (c h s)"
         turns = keep.tile([P, F_PASSES, 2, SEQ], F32)
-        nc.vector.tensor_scalar(
-            out=turns[:], in0=angle[:], scalar1=ROUND_TO_INT, scalar2=None, op0=ALU.add
-        )
-        minus_rest = keep.tile([P, F_PASSES, 2, SEQ], F32)
-        nc.vector.scalar_tensor_tensor(
-            out=minus_rest[:].rearrange(flat),
-            in0=turns[:].rearrange(flat),
-            scalar=ROUND_TO_INT,
-            in1=angle[:].rearrange(flat),
-            op0=ALU.subtract,
-            op1=ALU.subtract,
-        )
-        table = keep.tile([P, F_PASSES, SEQ, PACK], F32)
         for c in range(F_PASSES):
-            nc.scalar.activation(
-                out=table[:, c].rearrange("p s (h e) -> p s h e", e=2),
-                in_=minus_rest[:, c].rearrange("p h s -> p s h").unsqueeze(3).to_broadcast([P, SEQ, 2, 2]),
-                func=ACT.Sin,
-                scale=-TWO_PI,
+            nc.vector.tensor_scalar(
+                out=turns[:, c], in0=angle[:, c], scalar1=ROUND_TO_INT, scalar2=None, op0=ALU.add
             )
+        minus_rest = keep.tile([P, F_PASSES, 2, SEQ], F32)
+        for c in range(F_PASSES):
+            nc.vector.scalar_tensor_tensor(
+                out=minus_rest[:, c].rearrange("p h s -> p (h s)"),
+                in0=turns[:, c].rearrange("p h s -> p (h s)"),
+                scalar=ROUND_TO_INT,
+                in1=angle[:, c].rearrange("p h s -> p (h s)"),
+                op0=ALU.subtract,
+                op1=ALU.subtract,
+            )
+        table = keep.tile([P, F_PASSES, SEQ // RUN, PACK, RUN], F32)
+        for c in range(F_PASSES):
+            for h in range(2):
+                nc.scalar.activation(
+                    out=table[:, c, :, 2 * h : 2 * h + 2, :],
+                    in_=minus_rest[:, c, h, :]
+                    .rearrange("p (g r) -> p g r", r=RUN)
+                    .unsqueeze(2)
+                    .to_broadcast([P, SEQ // RUN, 2, RUN]),
+                    func=ACT.Sin,
+                    scale=-TWO_PI,
+                )
 
-        x_words = x_rows[:].bitcast(F32)
-        xT = transposed.tile([P, 2, TOKENS], F32, tag="bank")
-        for u in range(2):
-            nc.tensor.transpose(xT[:, u, :], x_words[:, u :: 2], identity[:])
         x_grouped = keep.tile([P, 2, TOKENS, PACK], BF16, align_bytes=64)
-        nc.vector.tensor_copy(
-            out=x_grouped[:, 1].bitcast(F32), in_=xT[:].rearrange("p u n -> p n u")
-        )
         x_codes = keep.tile([P, 3 * TOKENS], U32, align_bytes=64)
         x_scales = keep.tile([P, 3 * TOKENS], U8, align_bytes=64)
         minus_plus = slice(0, 2 * TOKENS)
         plus_plus = slice(TOKENS, 3 * TOKENS)
         last_copy = slice(2 * TOKENS, 3 * TOKENS)
-        nc.vector.tensor_scalar(
-            out=x_grouped[:, 0], in0=x_grouped[:, 1], scalar1=-1.0, scalar2=None, op0=ALU.mult
-        )
-        nc.vector.quantize_mx(
-            out=x_codes[:, last_copy].bitcast(FP8X4),
-            scales=x_scales[:, last_copy],
-            in_=x_grouped[:, 1].rearrange("p n t -> p (n t)"),
-        )
-        nc.vector.quantize_mx(
-            out=x_codes[:, minus_plus].bitcast(FP8X4),
-            scales=x_scales[:, minus_plus],
-            in_=x_grouped[:].rearrange("p a n t -> p (a n t)"),
-        )
+
+        def turn_x():
+            x_words = x_rows[:].bitcast(F32)
+            xT = transposed.tile([P, 2, TOKENS], F32, tag="bank")
+            for u in range(2):
+                nc.tensor.transpose(xT[:, u, :], x_words[:, u::2], identity[:])
+            nc.vector.tensor_copy(out=x_grouped[:, 1].bitcast(F32), in_=xT[:].rearrange("p u n -> p n u"))
+
+        def negate_x():
+            nc.vector.tensor_scalar(
+                out=x_grouped[:, 0], in0=x_grouped[:, 1], scalar1=-1.0, scalar2=None, op0=ALU.mult
+            )
+
+        def quantise_x():
+            nc.vector.quantize_mx(
+                out=x_codes[:, last_copy].bitcast(FP8X4),
+                scales=x_scales[:, last_copy],
+                in_=x_grouped[:, 1].rearrange("p n t -> p (n t)"),
+            )
+            nc.vector.quantize_mx(
+                out=x_codes[:, minus_plus].bitcast(FP8X4),
+                scales=x_scales[:, minus_plus],
+                in_=x_grouped[:].rearrange("p a n t -> p (a n t)"),
+            )
 
         w_words = w_rows[:].bitcast(F32)
         w_grouped = keep.tile([P, CHUNKS, PACK, P, PACK], BF16, align_bytes=64)
@@ -176,20 +187,22 @@ def tile_ropeattention_pa_s_kernel(tc, hidden_states, Wq, bq, Wk, bk, out):
         rot_codes = keep.tile([P, CHUNKS, TOKENS], U32, align_bytes=64)
         rot_scales = keep.tile([P, CHUNKS, TOKENS], U8, align_bytes=64)
 
-        def quantise_weights(i, copies):
-            halves = [slice(2 * h, 2 * h + 2) for h in range(2)]
-            for rows, copy in zip(halves, copies):
-                wT = transposed.tile([P, 2, 2, P], F32, tag="bank")
-                for e in range(2):
-                    for u in range(2):
-                        nc.tensor.transpose(wT[:, e, u, :], w_words[:, i, rows.start + e, u::2], identity[:])
-                copy(out=w_grouped[:, i, rows].bitcast(F32), in_=wT[:].rearrange("p e u m -> p e m u"))
-            for rows in halves:
-                nc.vector.quantize_mx(
-                    out=w_codes[:, i, rows].rearrange("p e m -> p (e m)").bitcast(FP8X4),
-                    scales=w_scales[:, i, rows].rearrange("p e m -> p (e m)"),
-                    in_=w_grouped[:, i, rows].rearrange("p e m t -> p (e m t)"),
-                )
+        def turn_weights(i, h, copy):
+            wT = transposed.tile([P, 2, 2, P], F32, tag="bank")
+            for e in range(2):
+                for u in range(2):
+                    nc.tensor.transpose(wT[:, e, u, :], w_words[:, i, 2 * h + e, u::2], identity[:])
+            copy(
+                out=w_grouped[:, i, 2 * h : 2 * h + 2].bitcast(F32), in_=wT[:].rearrange("p e u m -> p e m u")
+            )
+
+        def quantise_weights(i, h):
+            rows = slice(2 * h, 2 * h + 2)
+            nc.vector.quantize_mx(
+                out=w_codes[:, i, rows].rearrange("p e m -> p (e m)").bitcast(FP8X4),
+                scales=w_scales[:, i, rows].rearrange("p e m -> p (e m)"),
+                in_=w_grouped[:, i, rows].rearrange("p e m t -> p (e m t)"),
+            )
 
         bias_columns = keep.tile([P, CHUNKS, PACK], BF16)
         bias_rot = keep.tile([P, CHUNKS, PACK], F32)
@@ -225,10 +238,11 @@ def tile_ropeattention_pa_s_kernel(tc, hidden_states, Wq, bq, Wk, bk, out):
                     func=ACT.Identity,
                     bias=bias_rot[:, F_PASSES * (i % 2) + i // 2, t : t + 1],
                 )
+            runs = [P, BATCH, SEQ // RUN, PACK, RUN]
             nc.vector.tensor_tensor(
-                out=rot_grouped[:, i].rearrange("p (b s) t -> p b s t", b=BATCH),
-                in0=biased[:, i].rearrange("p t (b s) -> p b s t", b=BATCH),
-                in1=table[:, i // 2].unsqueeze(1).to_broadcast([P, BATCH, SEQ, PACK]),
+                out=rot_grouped[:, i].rearrange("p (b g r) t -> p b g t r", b=BATCH, r=RUN),
+                in0=biased[:, i].rearrange("p t (b g r) -> p b g t r", b=BATCH, r=RUN),
+                in1=table[:, i // 2].unsqueeze(1).to_broadcast(runs),
                 op=ALU.mult,
             )
 
@@ -239,18 +253,24 @@ def tile_ropeattention_pa_s_kernel(tc, hidden_states, Wq, bq, Wk, bk, out):
                 in_=rot_grouped[:, i].rearrange("p n t -> p (n t)"),
             )
 
-        on_scalar = (nc.scalar.copy, nc.scalar.copy)
-        on_both = (nc.scalar.copy, nc.vector.tensor_copy)
-        for i in range(LEAD):
-            quantise_weights(i, on_both if i >= 2 else on_scalar)
+        vector_copies = ((2, 1),)
+        for i in range(CHUNKS):
+            for h in range(2):
+                turn_weights(i, h, nc.vector.tensor_copy if (i, h) in vector_copies else nc.scalar.copy)
             if i == 0:
+                turn_x()
+            if i == 1:
                 turn_biases()
+            quantise_weights(i, 0)
+            if i == 0:
+                negate_x()
+            quantise_weights(i, 1)
+            if i == 0:
+                quantise_x()
         for i in range(CHUNKS):
             project_and_rotate(i)
             if i >= 1:
                 quantise_rotated(i - 1)
-            if i + LEAD < CHUNKS:
-                quantise_weights(i + LEAD, on_scalar)
         quantise_rotated(CHUNKS - 1)
 
         for c in range(F_PASSES):

@@ -41,8 +41,7 @@ def tile_ropeattention_pa_s_kernel(tc, hidden_states, Wq, bq, Wk, bk, out):
     with ExitStack() as ctx:
         ctx.enter_context(tc.manual_schedule())
         keep = ctx.enter_context(tc.tile_pool(name="keep", bufs=1))
-        transposed = ctx.enter_context(tc.psum_pool(name="transposed", bufs=4))
-        projected = ctx.enter_context(tc.psum_pool(name="projected", bufs=3))
+        banks = ctx.enter_context(tc.psum_pool(name="banks", bufs=7))
         scores = ctx.enter_context(tc.psum_pool(name="scores", bufs=1))
 
         ten_thousand = keep.tile([P, F_PASSES], F32)
@@ -156,7 +155,7 @@ def tile_ropeattention_pa_s_kernel(tc, hidden_states, Wq, bq, Wk, bk, out):
 
         def turn_x():
             x_words = x_rows[:].bitcast(F32)
-            xT = transposed.tile([P, 2, TOKENS], F32, tag="bank")
+            xT = banks.tile([P, 2, TOKENS], F32, tag="bank")
             for u in range(2):
                 nc.tensor.transpose(xT[:, u, :], x_words[:, u::2], identity[:])
             nc.vector.tensor_copy(out=x_grouped[:, 1].bitcast(F32), in_=xT[:].rearrange("p u n -> p n u"))
@@ -188,7 +187,7 @@ def tile_ropeattention_pa_s_kernel(tc, hidden_states, Wq, bq, Wk, bk, out):
         rot_scales = keep.tile([P, CHUNKS, TOKENS], U8, align_bytes=64)
 
         def turn_weights(i, h, copy):
-            wT = transposed.tile([P, 2, 2, P], F32, tag="bank")
+            wT = banks.tile([P, 2, 2, P], F32, tag="bank")
             for e in range(2):
                 for u in range(2):
                     nc.tensor.transpose(wT[:, e, u, :], w_words[:, i, 2 * h + e, u::2], identity[:])
@@ -209,7 +208,7 @@ def tile_ropeattention_pa_s_kernel(tc, hidden_states, Wq, bq, Wk, bk, out):
 
         def turn_biases():
             bias_words = bias_rows[:].bitcast(F32)
-            bT = transposed.tile([P, 2, P], F32, tag="bank")
+            bT = banks.tile([P, 2, P], F32, tag="bank")
             for u in range(2):
                 nc.tensor.transpose(bT[:, u, :], bias_words[:, u::2], identity[:])
             nc.scalar.copy(out=bias_columns[:].bitcast(F32), in_=bT[:, :, 0:CHUNKS].rearrange("p u r -> p r u"))
@@ -218,26 +217,30 @@ def tile_ropeattention_pa_s_kernel(tc, hidden_states, Wq, bq, Wk, bk, out):
             nc.gpsimd.tensor_tensor(out=rotated[:, :, 0], in0=pairs[:, :, 0], in1=pairs[:, :, 1], op=ALU.subtract)
             nc.gpsimd.tensor_tensor(out=rotated[:, :, 1], in0=pairs[:, :, 0], in1=pairs[:, :, 1], op=ALU.add)
 
-        def project_and_rotate(i):
-            y = projected.tile([P, PACK, TOKENS], F32)
-            for t in range(PACK):
-                moving = plus_plus if t % 2 == 0 else minus_plus
-                nc.tensor.matmul_mx(
-                    out=y[:, t - t % 2 : t - t % 2 + 2, :].rearrange("p e n -> p (e n)"),
-                    lhsT=w_codes[:, i, t, :].bitcast(FP8X4),
-                    lhsT_scale=w_scales[:, i, t, :],
-                    rhs=x_codes[:, moving].bitcast(FP8X4),
-                    rhs_scale=x_scales[:, moving],
-                    start=(t % 2 == 0),
-                    stop=(t % 2 == 1),
-                )
-            for t in range(PACK):
-                nc.scalar.activation(
-                    out=biased[:, i, t, :],
-                    in_=y[:, t, :],
-                    func=ACT.Identity,
-                    bias=bias_rot[:, F_PASSES * (i % 2) + i // 2, t : t + 1],
-                )
+        def project(i):
+            for h in range(2):
+                y = banks.tile([P, 2, TOKENS], F32, tag="bank")
+                for e in range(2):
+                    moving = plus_plus if e == 0 else minus_plus
+                    nc.tensor.matmul_mx(
+                        out=y[:].rearrange("p e n -> p (e n)"),
+                        lhsT=w_codes[:, i, 2 * h + e, :].bitcast(FP8X4),
+                        lhsT_scale=w_scales[:, i, 2 * h + e, :],
+                        rhs=x_codes[:, moving].bitcast(FP8X4),
+                        rhs_scale=x_scales[:, moving],
+                        start=(e == 0),
+                        stop=(e == 1),
+                    )
+                for e in range(2):
+                    t = 2 * h + e
+                    nc.scalar.activation(
+                        out=biased[:, i, t, :],
+                        in_=y[:, e, :],
+                        func=ACT.Identity,
+                        bias=bias_rot[:, F_PASSES * (i % 2) + i // 2, t : t + 1],
+                    )
+
+        def rotate(i):
             runs = [P, BATCH, SEQ // RUN, PACK, RUN]
             nc.vector.tensor_tensor(
                 out=rot_grouped[:, i].rearrange("p (b g r) t -> p b g t r", b=BATCH, r=RUN),
@@ -253,7 +256,7 @@ def tile_ropeattention_pa_s_kernel(tc, hidden_states, Wq, bq, Wk, bk, out):
                 in_=rot_grouped[:, i].rearrange("p n t -> p (n t)"),
             )
 
-        vector_copies = ((2, 1),)
+        vector_copies = ((CHUNKS - 1, 1),)
         for i in range(CHUNKS):
             for h in range(2):
                 turn_weights(i, h, nc.vector.tensor_copy if (i, h) in vector_copies else nc.scalar.copy)
@@ -268,7 +271,8 @@ def tile_ropeattention_pa_s_kernel(tc, hidden_states, Wq, bq, Wk, bk, out):
             if i == 0:
                 quantise_x()
         for i in range(CHUNKS):
-            project_and_rotate(i)
+            project(i)
+            rotate(i)
             if i >= 1:
                 quantise_rotated(i - 1)
         quantise_rotated(CHUNKS - 1)

import math
from contextlib import ExitStack

import concourse.mybir as mybir
from concourse.masks import make_identity

F32 = mybir.dt.float32
BF16 = mybir.dt.bfloat16
U32 = mybir.dt.uint32
U8 = mybir.dt.uint8
I32 = mybir.dt.int32
FP8X4 = mybir.dt.float8_e4m3fn_x4
ALU = mybir.AluOpType
ACT = mybir.ActivationFunctionType

P = 128
PACK = 4
K_PASS = P * PACK

BATCH, SEQ, D_IN, D_OUT = 2, 64, 512, 1024
TOKENS = BATCH * SEQ
HEAD = D_OUT // 2
F_PASSES = D_OUT // K_PASS
SIDES = ("q", "k")
CHUNKS = F_PASSES * len(SIDES)

RUN = 4
WARM_PASSES = 12

FLOPS = 2 * 2 * TOKENS * D_IN * D_OUT + 2 * BATCH * SEQ * SEQ * D_OUT

ROUND_TO_INT = 12582912.0
TWO_PI = 2.0 * math.pi


def tile_ropeattention_pa_s_kernel(tc, hidden_states, Wq, bq, Wk, bk, out):
    nc = tc.nc
    weights = {"q": Wq, "k": Wk}
    biases = {"q": bq, "k": bk}

    with ExitStack() as ctx:
        ctx.enter_context(tc.manual_schedule())
        keep = ctx.enter_context(tc.tile_pool(name="keep", bufs=1))
        banks = ctx.enter_context(tc.psum_pool(name="banks", bufs=7))
        scores = ctx.enter_context(tc.psum_pool(name="scores", bufs=1))

        ten_thousand = keep.tile([P, F_PASSES], F32)
        nc.vector.memset(ten_thousand[:], 10000.0)
        score = scores.tile([P, TOKENS], F32)
        zero_rows = keep.tile([P, K_PASS], BF16, align_bytes=64)
        idle_codes = keep.tile([P, TOKENS], U32, align_bytes=64)
        idle_scales = keep.tile([P, TOKENS], U8, align_bytes=64)
        nc.vector.memset(zero_rows[:].bitcast(I32), 0)
        nc.vector.quantize_mx(out=idle_codes[:].bitcast(FP8X4), scales=idle_scales[:], in_=zero_rows[:])
        bias_rows = keep.tile([P, K_PASS], BF16)
        nc.vector.memset(bias_rows[:].bitcast(I32), 0)

        for n in range(WARM_PASSES):
            nc.tensor.matmul_mx(
                out=score[:],
                lhsT=idle_codes[:].bitcast(FP8X4),
                lhsT_scale=idle_scales[:],
                rhs=idle_codes[:].bitcast(FP8X4),
                rhs_scale=idle_scales[:],
                start=True,
                stop=True,
            )

        x_rows = keep.tile([P, D_IN], BF16)
        w_rows = keep.tile([P, CHUNKS, PACK, D_IN], BF16)
        for i in range(CHUNKS):
            chunk_rows = weights[SIDES[i % 2]][(i // 2) * K_PASS : (i // 2 + 1) * K_PASS, :].rearrange(
                "(p t) d -> p t d", t=PACK
            )
            for h in range(2):
                nc.sync.dma_start(out=w_rows[:, i, 2 * h : 2 * h + 2, :], in_=chunk_rows[:, 2 * h : 2 * h + 2, :])
            if i == 0:
                nc.sync.dma_start(out=x_rows[:], in_=hidden_states.rearrange("b s d -> (b s) d"))
            if i == 1:
                for n, side in enumerate(SIDES):
                    nc.sync.dma_start(
                        out=bias_rows[F_PASSES * n : F_PASSES * (n + 1), :],
                        in_=biases[side].rearrange("(c k) -> c k", c=F_PASSES),
                    )

        exponent = keep.tile([P, F_PASSES], F32)
        nc.gpsimd.iota(
            exponent[:],
            pattern=[[P, F_PASSES]],
            base=0,
            channel_multiplier=1,
            allow_small_or_imprecise_dtypes=True,
        )
        nc.gpsimd.tensor_scalar(
            out=exponent[:], in0=exponent[:], scalar1=-2.0 / HEAD, scalar2=0.0, op0=ALU.mult, op1=ALU.add
        )
        position = keep.tile([P, SEQ], F32)
        nc.gpsimd.iota(
            position[:], pattern=[[1, SEQ]], base=0, channel_multiplier=0, allow_small_or_imprecise_dtypes=True
        )
        frequency = keep.tile([P, F_PASSES], F32)
        nc.gpsimd.tensor_tensor(out=frequency[:], in0=ten_thousand[:], in1=exponent[:], op=ALU.pow)
        identity = keep.tile([P, P], F32)
        make_identity(nc, identity[:])

        position_turns = keep.tile([P, SEQ], F32)
        nc.vector.tensor_scalar(
            out=position_turns[:], in0=position[:], scalar1=1.0 / TWO_PI, scalar2=None, op0=ALU.mult
        )
        angle = keep.tile([P, F_PASSES, 2, SEQ], F32)
        for c in range(F_PASSES):
            for h in range(2):
                nc.vector.tensor_scalar(
                    out=angle[:, c, h, :],
                    in0=position_turns[:],
                    scalar1=frequency[:, c : c + 1],
                    scalar2=h * 0.25,
                    op0=ALU.mult,
                    op1=ALU.add,
                )
        turns = keep.tile([P, F_PASSES, 2, SEQ], F32)
        for c in range(F_PASSES):
            nc.vector.tensor_scalar(
                out=turns[:, c], in0=angle[:, c], scalar1=ROUND_TO_INT, scalar2=None, op0=ALU.add
            )
        minus_rest = keep.tile([P, F_PASSES, 2, SEQ], F32)
        for c in range(F_PASSES):
            nc.vector.scalar_tensor_tensor(
                out=minus_rest[:, c].rearrange("p h s -> p (h s)"),
                in0=turns[:, c].rearrange("p h s -> p (h s)"),
                scalar=ROUND_TO_INT,
                in1=angle[:, c].rearrange("p h s -> p (h s)"),
                op0=ALU.subtract,
                op1=ALU.subtract,
            )
        table = keep.tile([P, F_PASSES, SEQ // RUN, PACK, RUN], F32)
        for c in range(F_PASSES):
            for h in range(2):
                nc.scalar.activation(
                    out=table[:, c, :, 2 * h : 2 * h + 2, :],
                    in_=minus_rest[:, c, h, :]
                    .rearrange("p (g r) -> p g r", r=RUN)
                    .unsqueeze(2)
                    .to_broadcast([P, SEQ // RUN, 2, RUN]),
                    func=ACT.Sin,
                    scale=-TWO_PI,
                )

        x_grouped = keep.tile([P, 2, TOKENS, PACK], BF16, align_bytes=64)
        x_codes = keep.tile([P, 3 * TOKENS], U32, align_bytes=64)
        x_scales = keep.tile([P, 3 * TOKENS], U8, align_bytes=64)
        minus_plus = slice(0, 2 * TOKENS)
        plus_plus = slice(TOKENS, 3 * TOKENS)
        last_copy = slice(2 * TOKENS, 3 * TOKENS)

        def turn_x():
            x_words = x_rows[:].bitcast(F32)
            xT = banks.tile([P, 2, TOKENS], F32, tag="bank")
            for u in range(2):
                nc.tensor.transpose(xT[:, u, :], x_words[:, u::2], identity[:])
            nc.vector.tensor_copy(out=x_grouped[:, 1].bitcast(F32), in_=xT[:].rearrange("p u n -> p n u"))

        def negate_x():
            nc.vector.tensor_scalar(
                out=x_grouped[:, 0], in0=x_grouped[:, 1], scalar1=-1.0, scalar2=None, op0=ALU.mult
            )

        def quantise_x():
            nc.vector.quantize_mx(
                out=x_codes[:, last_copy].bitcast(FP8X4),
                scales=x_scales[:, last_copy],
                in_=x_grouped[:, 1].rearrange("p n t -> p (n t)"),
            )
            nc.vector.quantize_mx(
                out=x_codes[:, minus_plus].bitcast(FP8X4),
                scales=x_scales[:, minus_plus],
                in_=x_grouped[:].rearrange("p a n t -> p (a n t)"),
            )

        w_words = w_rows[:].bitcast(F32)
        w_grouped = keep.tile([P, CHUNKS, PACK, P, PACK], BF16, align_bytes=64)
        w_codes = keep.tile([P, CHUNKS, PACK, P], U32, align_bytes=64)
        w_scales = keep.tile([P, CHUNKS, PACK, P], U8, align_bytes=64)
        biased = keep.tile([P, CHUNKS, PACK, TOKENS], F32)
        rot_grouped = keep.tile([P, CHUNKS, TOKENS, PACK], BF16, align_bytes=64)
        rot_codes = keep.tile([P, CHUNKS, TOKENS], U32, align_bytes=64)
        rot_scales = keep.tile([P, CHUNKS, TOKENS], U8, align_bytes=64)

        def turn_weights(i, h, copy):
            wT = banks.tile([P, 2, 2, P], F32, tag="bank")
            for e in range(2):
                for u in range(2):
                    nc.tensor.transpose(wT[:, e, u, :], w_words[:, i, 2 * h + e, u::2], identity[:])
            copy(
                out=w_grouped[:, i, 2 * h : 2 * h + 2].bitcast(F32), in_=wT[:].rearrange("p e u m -> p e m u")
            )

        def quantise_weights(i, h):
            rows = slice(2 * h, 2 * h + 2)
            nc.vector.quantize_mx(
                out=w_codes[:, i, rows].rearrange("p e m -> p (e m)").bitcast(FP8X4),
                scales=w_scales[:, i, rows].rearrange("p e m -> p (e m)"),
                in_=w_grouped[:, i, rows].rearrange("p e m t -> p (e m t)"),
            )

        bias_columns = keep.tile([P, CHUNKS, PACK], BF16)
        bias_rot = keep.tile([P, CHUNKS, PACK], F32)

        def turn_biases():
            bias_words = bias_rows[:].bitcast(F32)
            bT = banks.tile([P, 2, P], F32, tag="bank")
            for u in range(2):
                nc.tensor.transpose(bT[:, u, :], bias_words[:, u::2], identity[:])
            nc.scalar.copy(out=bias_columns[:].bitcast(F32), in_=bT[:, :, 0:CHUNKS].rearrange("p u r -> p r u"))
            pairs = bias_columns[:].rearrange("p r (h e) -> p (r h) e", e=2)
            rotated = bias_rot[:].rearrange("p r (h e) -> p (r h) e", e=2)
            nc.gpsimd.tensor_tensor(out=rotated[:, :, 0], in0=pairs[:, :, 0], in1=pairs[:, :, 1], op=ALU.subtract)
            nc.gpsimd.tensor_tensor(out=rotated[:, :, 1], in0=pairs[:, :, 0], in1=pairs[:, :, 1], op=ALU.add)

        def project(i):
            for h in range(2):
                y = banks.tile([P, 2, TOKENS], F32, tag="bank")
                for e in range(2):
                    moving = plus_plus if e == 0 else minus_plus
                    nc.tensor.matmul_mx(
                        out=y[:].rearrange("p e n -> p (e n)"),
                        lhsT=w_codes[:, i, 2 * h + e, :].bitcast(FP8X4),
                        lhsT_scale=w_scales[:, i, 2 * h + e, :],
                        rhs=x_codes[:, moving].bitcast(FP8X4),
                        rhs_scale=x_scales[:, moving],
                        start=(e == 0),
                        stop=(e == 1),
                    )
                for e in range(2):
                    t = 2 * h + e
                    nc.scalar.activation(
                        out=biased[:, i, t, :],
                        in_=y[:, e, :],
                        func=ACT.Identity,
                        bias=bias_rot[:, F_PASSES * (i % 2) + i // 2, t : t + 1],
                    )

        def rotate(i):
            runs = [P, BATCH, SEQ // RUN, PACK, RUN]
            nc.vector.tensor_tensor(
                out=rot_grouped[:, i].rearrange("p (b g r) t -> p b g t r", b=BATCH, r=RUN),
                in0=biased[:, i].rearrange("p t (b g r) -> p b g t r", b=BATCH, r=RUN),
                in1=table[:, i // 2].unsqueeze(1).to_broadcast(runs),
                op=ALU.mult,
            )

        def quantise_rotated(i):
            nc.vector.quantize_mx(
                out=rot_codes[:, i, :].bitcast(FP8X4),
                scales=rot_scales[:, i, :],
                in_=rot_grouped[:, i].rearrange("p n t -> p (n t)"),
            )

        vector_copies = ((CHUNKS - 1, 1),)
        for i in range(CHUNKS):
            for h in range(2):
                turn_weights(i, h, nc.vector.tensor_copy if (i, h) in vector_copies else nc.scalar.copy)
            if i == 0:
                turn_x()
            if i == 1:
                turn_biases()
            quantise_weights(i, 0)
            if i == 0:
                negate_x()
            quantise_weights(i, 1)
            if i == 0:
                quantise_x()
        for i in range(CHUNKS):
            project(i)
            rotate(i)
            if i >= 1:
                quantise_rotated(i - 1)
        quantise_rotated(CHUNKS - 1)

        for c in range(F_PASSES):
            nc.tensor.matmul_mx(
                out=score[:],
                lhsT=rot_codes[:, 2 * c, :].bitcast(FP8X4),
                lhsT_scale=rot_scales[:, 2 * c, :],
                rhs=rot_codes[:, 2 * c + 1, :].bitcast(FP8X4),
                rhs_scale=rot_scales[:, 2 * c + 1, :],
                start=(c == 0),
                stop=(c == F_PASSES - 1),
            )

        scaled = keep.tile([P, SEQ], F32)
        nc.vector.tensor_scalar(
            out=scaled[0:SEQ, :], in0=score[0:SEQ, 0:SEQ], scalar1=1.0 / math.sqrt(HEAD), scalar2=None, op0=ALU.mult
        )
        nc.vector.tensor_scalar(
            out=scaled[SEQ:P, :], in0=score[SEQ:P, SEQ:P], scalar1=1.0 / math.sqrt(HEAD), scalar2=None, op0=ALU.mult
        )
        nc.sync.dma_start(out=out.rearrange("b s j -> (b s) j"), in_=scaled[:])
